import numpy as np
import ml_dtypes


def mxq(x, axis, fmt="e4m3"):
    dtype, down = {"e4m3": (ml_dtypes.float8_e4m3fn, 7), "e5m2": (ml_dtypes.float8_e5m2, 14)}[fmt]
    v = np.moveaxis(np.asarray(x, np.float32).astype(ml_dtypes.bfloat16).astype(np.float64), axis, -1)
    blocks = v.reshape(v.shape[:-1] + (-1, 32))
    amax = np.abs(blocks).max(-1, keepdims=True)
    byte = np.maximum(np.where(amax > 0, np.frexp(amax)[1] - 1 + 127, 0) - down, 1)
    scale = np.exp2(byte - 127.0)
    codes = (blocks / scale).astype(np.float32).astype(dtype).astype(np.float64)
    return np.moveaxis((codes * scale).reshape(v.shape), -1, axis)


WIDE = False


def mx_kscale(k):
    if not WIDE:
        return np.ones(k)
    levels = np.array([10, -10, 5, -5, 0])
    a = np.random.permutation(np.resize(levels, k // 512 * 4)).reshape(k // 512, 4)
    idx = np.arange(k)
    return np.exp2(a[idx // 512, idx % 128 // 32])


BF16 = ml_dtypes.bfloat16


def bf(x):
    return np.asarray(x, np.float32).astype(BF16)


def f64(x):
    return np.asarray(x).astype(np.float64)


B, C, H, W, HID, VOCAB = 128, 3, 84, 84, 1024, 1024
EPS = 1e-8
BETA = 8


def setup_inputs():
    words = np.random.standard_normal((VOCAB, HID))
    gain = 0.5 + np.random.random((VOCAB, 1))
    near = np.random.randint(0, VOCAB, B)
    a = 0.6 + 0.35 * np.random.random((B, 1))
    q = 1.5 * (a * words[near] + np.sqrt(1.0 - a * a) * np.random.standard_normal((B, HID)))
    r = mx_kscale(HID)[np.arange(B) * HID // B][:, None]
    return {"q": bf(q * r), "word_embs": bf(words * gain), "beta": BETA}


def reference(q, word_embs, beta):
    q, e = f64(q), f64(word_embs)
    q_norm = np.sqrt((q * q).sum(-1, keepdims=True))
    e_norm = np.sqrt((e * e).sum(-1))[None, :]
    sims = (mxq(q, 1, "e4m3") @ mxq(e, 1, "e4m3").T) / (q_norm * e_norm + EPS)
    x = beta * sims
    p = np.exp(x - x.max(-1, keepdims=True))
    return (mxq(p, 1, "e4m3") @ mxq(e, 0, "e4m3")) / p.sum(-1, keepdims=True)

@@ -1,0 +1,248 @@
+from contextlib import ExitStack
+
+import concourse.mybir as mybir
+from concourse.masks import make_identity
+
+F32 = mybir.dt.float32
+BF16 = mybir.dt.bfloat16
+U32 = mybir.dt.uint32
+U8 = mybir.dt.uint8
+FP8X4 = mybir.dt.float8_e4m3fn_x4
+ALU = mybir.AluOpType
+ACT = mybir.ActivationFunctionType
+
+P = 128
+PACK = 4
+K_PASS = P * PACK
+QUERIES = 128
+HID = 1024
+VOCAB = 1024
+H_PASSES = HID // K_PASS
+V_PASSES = VOCAB // K_PASS
+CHUNKS = VOCAB // P
+BANK = 512
+EPS = 1e-8
+
+FLOPS = 2 * 2 * QUERIES * VOCAB * HID
+
+
+def tile_frozenhopfield_pa_s_kernel(tc, q, word_embs, beta, out):
+    nc = tc.nc
+    with ExitStack() as pools:
+        keep = pools.enter_context(tc.tile_pool(name="keep", bufs=1))
+        turn_ps = pools.enter_context(tc.psum_pool(name="turn_ps", bufs=4))
+        hold_ps = pools.enter_context(tc.psum_pool(name="hold_ps", bufs=1))
+
+        q_rows = keep.tile([P, HID], BF16, align_bytes=64)
+        nc.sync.dma_start(out=q_rows[:], in_=q[:, :])
+        e_rows = keep.tile([P, V_PASSES, PACK, HID], BF16, align_bytes=64)
+        e_dram = word_embs.rearrange("(g p j) h -> p g j h", g=V_PASSES, p=P, j=PACK)
+        for g in range(V_PASSES):
+            for j in range(PACK):
+                nc.sync.dma_start(out=e_rows[:, g, j, :], in_=e_dram[:, g, j, :])
+
+        ident = keep.tile([P, P], F32)
+        make_identity(nc, ident[:])
+
+        ones = keep.tile([P, 1], F32)
+        nc.vector.memset(ones[:], 1.0)
+        warm_sqrt = keep.tile([P, 1], F32)
+        nc.scalar.activation(out=warm_sqrt[:], in_=ones[:], func=ACT.Sqrt)
+
+        squares = keep.tile([P, CHUNKS + 1, HID], BF16)
+        q_sq = keep.tile([P, 1], F32)
+        q_norm = keep.tile([P, 1], F32)
+        e_sq = keep.tile([P, CHUNKS], F32)
+        e_norm = keep.tile([P, CHUNKS], F32)
+
+        q_grouped = keep.tile([P, HID], BF16, align_bytes=64)
+        q_codes = keep.tile([P, H_PASSES, P], U32, align_bytes=64)
+        q_scales = keep.tile([P, H_PASSES, P], U8, align_bytes=64)
+        et_grouped = keep.tile([P, CHUNKS, HID], BF16, align_bytes=64)
+        et_codes = keep.tile([P, CHUNKS, H_PASSES, P], U32, align_bytes=64)
+        et_scales = keep.tile([P, CHUNKS, H_PASSES, P], U8, align_bytes=64)
+        e2_grouped = keep.tile([P, V_PASSES, HID, PACK], BF16, align_bytes=64)
+        e2_codes = keep.tile([P, V_PASSES, HID], U32, align_bytes=64)
+        e2_scales = keep.tile([P, V_PASSES, HID], U8, align_bytes=64)
+
+        def turn_features(rows):
+            words = rows.bitcast(F32)
+            turned = turn_ps.tile([P, H_PASSES, 2, P], F32, tag="turned")
+            for s in range(H_PASSES):
+                for u in range(2):
+                    first = (2 * s + u) * P
+                    nc.tensor.transpose(turned[:, s, u, :], words[:, first : first + P], ident[:])
+            return turned
+
+        def grouped_view(grouped):
+            return grouped.bitcast(F32).rearrange("p (s r u) -> p s r u", s=H_PASSES, u=2)
+
+        q_turned = turn_features(q_rows[:])
+        nc.vector.tensor_copy(
+            out=grouped_view(q_grouped[:]), in_=q_turned[:].rearrange("p s u r -> p s r u")
+        )
+        nc.scalar.activation(
+            out=squares[:, CHUNKS, :], in_=q_rows[:], func=ACT.Square, accum_out=q_sq[:]
+        )
+        nc.scalar.activation(out=q_norm[:], in_=q_sq[:], func=ACT.Sqrt)
+        nc.vector.quantize_mx(
+            out=q_codes[:].rearrange("p s r -> p (s r)").bitcast(FP8X4),
+            scales=q_scales[:].rearrange("p s r -> p (s r)"),
+            in_=q_grouped[:],
+        )
+        spread = turn_ps.tile([P, P], F32, tag="turned")
+        nc.tensor.matmul(
+            out=spread[:], lhsT=q_norm[:, 0:1].to_broadcast([P, P]), rhs=ident[:], start=True, stop=True
+        )
+        q_norm_cols = keep.tile([P, QUERIES], F32)
+        nc.vector.tensor_scalar(
+            out=q_norm_cols[:], in0=spread[:], scalar1=1.0 / beta, scalar2=None, op0=ALU.mult
+        )
+
+        dots = [hold_ps.tile([P, BANK], F32, name="dots%d" % g) for g in range(V_PASSES)]
+        dens = [hold_ps.tile([P, BANK], F32, name="dens%d" % i) for i in range(2)]
+        den_t = keep.tile([P, CHUNKS, QUERIES], F32)
+        scale = keep.tile([P, VOCAB], F32)
+        x = keep.tile([P, VOCAB], F32)
+        part_max = keep.tile([P, V_PASSES], F32)
+
+        def den_bank(c):
+            return dens[c % 2][:, (c // 2) * P : (c // 2 + 1) * P]
+
+        def regroup(g, half):
+            cols = slice(half * BANK, (half + 1) * BANK)
+            nc.vector.tensor_copy(
+                out=e2_grouped[:, g, cols, :].rearrange("p (c i) j -> p c j i", i=4),
+                in_=e_rows[:, g, :, cols].rearrange("p j (c i) -> p c j i", i=4),
+            )
+
+        def quantise_words(g, half):
+            cols = slice(half * BANK, (half + 1) * BANK)
+            nc.vector.quantize_mx(
+                out=e2_codes[:, g, cols].bitcast(FP8X4),
+                scales=e2_scales[:, g, cols],
+                in_=e2_grouped[:, g, cols, :].rearrange("p h j -> p (h j)"),
+            )
+
+        def invert(c):
+            nc.vector.reciprocal(out=scale[:, c * P : (c + 1) * P], in_=den_bank(c))
+
+        def scaled_sims(g):
+            cols = slice(g * BANK, (g + 1) * BANK)
+            nc.vector.tensor_tensor(out=x[:, cols], in0=dots[g][:], in1=scale[:, cols], op=ALU.mult)
+            nc.vector.tensor_reduce(
+                out=part_max[:, g : g + 1], in_=x[:, cols], axis=mybir.AxisListType.X, op=ALU.max
+            )
+
+        turned = turn_features(e_rows[:, 0, 0, :])
+        for c in range(CHUNKS):
+            g, j = divmod(c, PACK)
+            this_turned = turned
+            if c + 1 < CHUNKS:
+                turned = turn_features(e_rows[:, (c + 1) // PACK, (c + 1) % PACK, :])
+            nc.scalar.copy(
+                out=grouped_view(et_grouped[:, c, :]),
+                in_=this_turned[:].rearrange("p s u r -> p s r u"),
+            )
+            nc.scalar.activation(
+                out=squares[:, c, :], in_=e_rows[:, g, j, :], func=ACT.Square,
+                accum_out=e_sq[:, c : c + 1],
+            )
+            nc.scalar.activation(out=e_norm[:, c : c + 1], in_=e_sq[:, c : c + 1], func=ACT.Sqrt)
+            nc.vector.quantize_mx(
+                out=et_codes[:, c, :, :].rearrange("p s r -> p (s r)").bitcast(FP8X4),
+                scales=et_scales[:, c, :, :].rearrange("p s r -> p (s r)"),
+                in_=et_grouped[:, c, :],
+            )
+            for s in range(H_PASSES):
+                nc.tensor.matmul_mx(
+                    out=dots[g][:, j * P : (j + 1) * P],
+                    lhsT=q_codes[:, s, :].bitcast(FP8X4),
+                    lhsT_scale=q_scales[:, s, :],
+                    rhs=et_codes[:, c, s, :].bitcast(FP8X4),
+                    rhs_scale=et_scales[:, c, s, :],
+                    start=(s == 0),
+                    stop=(s == H_PASSES - 1),
+                )
+            nc.vector.tensor_scalar(
+                out=den_t[:, c, :], in0=q_norm_cols[:], scalar1=e_norm[:, c : c + 1],
+                scalar2=EPS / beta, op0=ALU.mult, op1=ALU.add,
+            )
+            nc.tensor.transpose(den_bank(c), den_t[:, c, :], ident[:])
+            if c > 0:
+                invert(c - 1)
+            if c == PACK + 1:
+                scaled_sims(0)
+            if c % 2 == 0:
+                regroup(c // 4, (c // 2) % 2)
+            else:
+                quantise_words(c // 4, (c // 2) % 2)
+        invert(CHUNKS - 1)
+        scaled_sims(1)
+
+        warm_exp = keep.tile([P, 1], F32)
+        nc.scalar.activation(
+            out=warm_exp[:], in_=e_norm[:, CHUNKS - 1 : CHUNKS], func=ACT.Exp, scale=0.0
+        )
+
+        neg_max = keep.tile([P, 1], F32)
+        nc.vector.tensor_reduce(
+            out=neg_max[:], in_=part_max[:], axis=mybir.AxisListType.X, op=ALU.max, negate=True
+        )
+        prob = keep.tile([P, VOCAB], F32)
+        part_sum = keep.tile([P, V_PASSES], F32)
+        p_grouped = keep.tile([P, V_PASSES, QUERIES, PACK], BF16, align_bytes=64)
+        p_codes = keep.tile([P, V_PASSES, QUERIES], U32, align_bytes=64)
+        p_scales = keep.tile([P, V_PASSES, QUERIES], U8, align_bytes=64)
+        for g in range(V_PASSES):
+            cols = slice(g * BANK, (g + 1) * BANK)
+            nc.scalar.activation(
+                out=prob[:, cols], in_=x[:, cols], func=ACT.Exp, bias=neg_max[:, 0:1], scale=1.0,
+                accum_out=part_sum[:, g : g + 1],
+            )
+        for g in range(V_PASSES):
+            p_turned = turn_ps.tile([P, PACK, QUERIES], F32, tag="turned")
+            for j in range(PACK):
+                first = (g * PACK + j) * P
+                nc.tensor.transpose(p_turned[:, j, :], prob[:, first : first + P], ident[:])
+            if g == 0:
+                nc.vector.tensor_copy(
+                    out=p_grouped[:, g, :, :], in_=p_turned[:].rearrange("p j b -> p b j")
+                )
+            else:
+                nc.scalar.copy(out=p_grouped[:, g, :, :], in_=p_turned[:].rearrange("p j b -> p b j"))
+        for g in range(V_PASSES):
+            nc.vector.quantize_mx(
+                out=p_codes[:, g, :].bitcast(FP8X4),
+                scales=p_scales[:, g, :],
+                in_=p_grouped[:, g, :, :].rearrange("p b j -> p (b j)"),
+            )
+        row_sum = keep.tile([P, 1], F32)
+        nc.vector.tensor_reduce(
+            out=row_sum[:], in_=part_sum[:], axis=mybir.AxisListType.X, op=ALU.add
+        )
+        inv_sum = keep.tile([P, 1], F32)
+        nc.vector.reciprocal(out=inv_sum[:], in_=row_sum[:])
+
+        for n in range(HID // BANK):
+            cols = slice(n * BANK, (n + 1) * BANK)
+            acc = hold_ps.tile([P, BANK], F32, name="acc%d" % n, tag="dots%d" % n)
+            for g in range(V_PASSES):
+                nc.tensor.matmul_mx(
+                    out=acc[:],
+                    lhsT=p_codes[:, g, :].bitcast(FP8X4),
+                    lhsT_scale=p_scales[:, g, :],
+                    rhs=e2_codes[:, g, cols].bitcast(FP8X4),
+                    rhs_scale=e2_scales[:, g, cols],
+                    start=(g == 0),
+                    stop=(g == V_PASSES - 1),
+                )
+            result = keep.tile([P, BANK], F32, name="result%d" % n)
+            if n == 0:
+                nc.vector.tensor_scalar(
+                    out=result[:], in0=acc[:], scalar1=inv_sum[:, 0:1], scalar2=None, op0=ALU.mult
+                )
+                nc.sync.dma_start(out=out[:, cols], in_=result[:])
+            else:
+                nc.scalar.activation(out=result[:], in_=acc[:], func=ACT.Copy, scale=inv_sum[:, 0:1])
+                nc.scalar.dma_start(out=out[:, cols], in_=result[:])

@@ -111,9 +111,10 @@ def tile_frozenhopfield_pa_s_kernel(tc, q, word_embs, beta, out):
 
         def regroup(g, half):
             cols = slice(half * BANK, (half + 1) * BANK)
-            nc.vector.tensor_copy(
+            nc.gpsimd.tensor_scalar(
                 out=e2_grouped[:, g, cols, :].rearrange("p (c i) j -> p c j i", i=4),
-                in_=e_rows[:, g, :, cols].rearrange("p j (c i) -> p c j i", i=4),
+                in0=e_rows[:, g, :, cols].rearrange("p j (c i) -> p c j i", i=4),
+                scalar1=1.0, scalar2=0.0, op0=ALU.mult, op1=ALU.add,
             )
 
         def quantise_words(g, half):

@@ -10,6 +10,7 @@ U8 = mybir.dt.uint8
 FP8X4 = mybir.dt.float8_e4m3fn_x4
 ALU = mybir.AluOpType
 ACT = mybir.ActivationFunctionType
+ROW = mybir.AxisListType.X
 
 P = 128
 PACK = 4
@@ -21,7 +22,9 @@ H_PASSES = HID // K_PASS
 V_PASSES = VOCAB // K_PASS
 CHUNKS = VOCAB // P
 BANK = 512
+QUARTER = HID // PACK
 EPS = 1e-8
+VECTOR_COPIES = 2
 
 FLOPS = 2 * 2 * QUERIES * VOCAB * HID
 
@@ -32,6 +35,7 @@ def tile_frozenhopfield_pa_s_kernel(tc, q, word_embs, beta, out):
         keep = pools.enter_context(tc.tile_pool(name="keep", bufs=1))
         turn_ps = pools.enter_context(tc.psum_pool(name="turn_ps", bufs=4))
         hold_ps = pools.enter_context(tc.psum_pool(name="hold_ps", bufs=1))
+        pools.enter_context(tc.manual_schedule())
 
         q_rows = keep.tile([P, HID], BF16, align_bytes=64)
         nc.sync.dma_start(out=q_rows[:], in_=q[:, :])
@@ -43,11 +47,12 @@ def tile_frozenhopfield_pa_s_kernel(tc, q, word_embs, beta, out):
 
         ident = keep.tile([P, P], F32)
         make_identity(nc, ident[:])
+        half = keep.tile([P, 1], F32)
+        nc.gpsimd.memset(half[:], 0.5)
 
-        ones = keep.tile([P, 1], F32)
-        nc.vector.memset(ones[:], 1.0)
-        warm_sqrt = keep.tile([P, 1], F32)
-        nc.scalar.activation(out=warm_sqrt[:], in_=ones[:], func=ACT.Sqrt)
+        warm = keep.tile([P, 1], F32)
+        nc.vector.memset(warm[:], 0.0)
+        nc.scalar.activation(out=warm[:], in_=warm[:], func=ACT.Exp)
 
         squares = keep.tile([P, CHUNKS + 1, HID], BF16)
         q_sq = keep.tile([P, 1], F32)
@@ -65,91 +70,34 @@ def tile_frozenhopfield_pa_s_kernel(tc, q, word_embs, beta, out):
         e2_codes = keep.tile([P, V_PASSES, HID], U32, align_bytes=64)
         e2_scales = keep.tile([P, V_PASSES, HID], U8, align_bytes=64)
 
-        def turn_features(rows):
-            words = rows.bitcast(F32)
-            turned = turn_ps.tile([P, H_PASSES, 2, P], F32, tag="turned")
-            for s in range(H_PASSES):
-                for u in range(2):
-                    first = (2 * s + u) * P
-                    nc.tensor.transpose(turned[:, s, u, :], words[:, first : first + P], ident[:])
-            return turned
-
-        def grouped_view(grouped):
-            return grouped.bitcast(F32).rearrange("p (s r u) -> p s r u", s=H_PASSES, u=2)
-
-        q_turned = turn_features(q_rows[:])
-        nc.vector.tensor_copy(
-            out=grouped_view(q_grouped[:]), in_=q_turned[:].rearrange("p s u r -> p s r u")
-        )
-        nc.scalar.activation(
-            out=squares[:, CHUNKS, :], in_=q_rows[:], func=ACT.Square, accum_out=q_sq[:]
-        )
-        nc.scalar.activation(out=q_norm[:], in_=q_sq[:], func=ACT.Sqrt)
-        nc.vector.quantize_mx(
-            out=q_codes[:].rearrange("p s r -> p (s r)").bitcast(FP8X4),
-            scales=q_scales[:].rearrange("p s r -> p (s r)"),
-            in_=q_grouped[:],
-        )
-        spread = turn_ps.tile([P, P], F32, tag="turned")
-        nc.tensor.matmul(
-            out=spread[:], lhsT=q_norm[:, 0:1].to_broadcast([P, P]), rhs=ident[:], start=True, stop=True
-        )
         q_norm_cols = keep.tile([P, QUERIES], F32)
-        nc.vector.tensor_scalar(
-            out=q_norm_cols[:], in0=spread[:], scalar1=1.0 / beta, scalar2=None, op0=ALU.mult
-        )
-
         dots = [hold_ps.tile([P, BANK], F32, name="dots%d" % g) for g in range(V_PASSES)]
         dens = [hold_ps.tile([P, BANK], F32, name="dens%d" % i) for i in range(2)]
         den_t = keep.tile([P, CHUNKS, QUERIES], F32)
         scale = keep.tile([P, VOCAB], F32)
         x = keep.tile([P, VOCAB], F32)
         part_max = keep.tile([P, V_PASSES], F32)
+        turned = {}
 
-        def den_bank(c):
-            return dens[c % 2][:, (c // 2) * P : (c // 2 + 1) * P]
+        def chunk_rows(c):
+            return e_rows[:, c // PACK, c % PACK, :]
 
-        def regroup(g, half):
-            cols = slice(half * BANK, (half + 1) * BANK)
-            nc.gpsimd.tensor_scalar(
-                out=e2_grouped[:, g, cols, :].rearrange("p (c i) j -> p c j i", i=4),
-                in0=e_rows[:, g, :, cols].rearrange("p j (c i) -> p c j i", i=4),
-                scalar1=1.0, scalar2=0.0, op0=ALU.mult, op1=ALU.add,
+        def turn_features(name, rows):
+            words = rows.bitcast(F32)
+            bank = turn_ps.tile([P, H_PASSES, 2, P], F32, tag="turned", name="turned_%s" % name)
+            for s in range(H_PASSES):
+                for u in range(2):
+                    first = (2 * s + u) * P
+                    nc.tensor.transpose(bank[:, s, u, :], words[:, first : first + P], ident[:])
+            turned[name] = bank
+
+        def copy_out(copy, name, grouped):
+            copy(
+                out=grouped.bitcast(F32).rearrange("p (s r u) -> p s r u", s=H_PASSES, u=2),
+                in_=turned[name][:].rearrange("p s u r -> p s r u"),
             )
 
-        def quantise_words(g, half):
-            cols = slice(half * BANK, (half + 1) * BANK)
-            nc.vector.quantize_mx(
-                out=e2_codes[:, g, cols].bitcast(FP8X4),
-                scales=e2_scales[:, g, cols],
-                in_=e2_grouped[:, g, cols, :].rearrange("p h j -> p (h j)"),
-            )
-
-        def invert(c):
-            nc.vector.reciprocal(out=scale[:, c * P : (c + 1) * P], in_=den_bank(c))
-
-        def scaled_sims(g):
-            cols = slice(g * BANK, (g + 1) * BANK)
-            nc.vector.tensor_tensor(out=x[:, cols], in0=dots[g][:], in1=scale[:, cols], op=ALU.mult)
-            nc.vector.tensor_reduce(
-                out=part_max[:, g : g + 1], in_=x[:, cols], axis=mybir.AxisListType.X, op=ALU.max
-            )
-
-        turned = turn_features(e_rows[:, 0, 0, :])
-        for c in range(CHUNKS):
-            g, j = divmod(c, PACK)
-            this_turned = turned
-            if c + 1 < CHUNKS:
-                turned = turn_features(e_rows[:, (c + 1) // PACK, (c + 1) % PACK, :])
-            nc.scalar.copy(
-                out=grouped_view(et_grouped[:, c, :]),
-                in_=this_turned[:].rearrange("p s u r -> p s r u"),
-            )
-            nc.scalar.activation(
-                out=squares[:, c, :], in_=e_rows[:, g, j, :], func=ACT.Square,
-                accum_out=e_sq[:, c : c + 1],
-            )
-            nc.scalar.activation(out=e_norm[:, c : c + 1], in_=e_sq[:, c : c + 1], func=ACT.Sqrt)
+        def quantise_chunk(c):
             nc.vector.quantize_mx(
                 out=et_codes[:, c, :, :].rearrange("p s r -> p (s r)").bitcast(FP8X4),
                 scales=et_scales[:, c, :, :].rearrange("p s r -> p (s r)"),
@@ -157,7 +105,7 @@ def tile_frozenhopfield_pa_s_kernel(tc, q, word_embs, beta, out):
             )
             for s in range(H_PASSES):
                 nc.tensor.matmul_mx(
-                    out=dots[g][:, j * P : (j + 1) * P],
+                    out=dots[c // PACK][:, (c % PACK) * P : (c % PACK + 1) * P],
                     lhsT=q_codes[:, s, :].bitcast(FP8X4),
                     lhsT_scale=q_scales[:, s, :],
                     rhs=et_codes[:, c, s, :].bitcast(FP8X4),
@@ -165,31 +113,88 @@ def tile_frozenhopfield_pa_s_kernel(tc, q, word_embs, beta, out):
                     start=(s == 0),
                     stop=(s == H_PASSES - 1),
                 )
-            nc.vector.tensor_scalar(
+
+        def den_bank(c):
+            return dens[c % 2][:, (c // 2) * P : (c // 2 + 1) * P]
+
+        def denominators(c):
+            nc.scalar.activation(
+                out=squares[:, c, :], in_=chunk_rows(c), func=ACT.Square, accum_out=e_sq[:, c : c + 1]
+            )
+            nc.gpsimd.tensor_tensor(
+                out=e_norm[:, c : c + 1], in0=e_sq[:, c : c + 1], in1=half[:], op=ALU.pow
+            )
+            nc.gpsimd.tensor_scalar(
                 out=den_t[:, c, :], in0=q_norm_cols[:], scalar1=e_norm[:, c : c + 1],
                 scalar2=EPS / beta, op0=ALU.mult, op1=ALU.add,
             )
             nc.tensor.transpose(den_bank(c), den_t[:, c, :], ident[:])
-            if c > 0:
-                invert(c - 1)
-            if c == PACK + 1:
+
+        def regroup(copy, g, part):
+            cols = slice(part * QUARTER, (part + 1) * QUARTER)
+            copy(
+                out=e2_grouped[:, g, cols, :].rearrange("p (c i) j -> p c j i", i=4),
+                in_=e_rows[:, g, :, cols].rearrange("p j (c i) -> p c j i", i=4),
+            )
+
+        def quantise_words(g, n):
+            cols = slice(n * BANK, (n + 1) * BANK)
+            nc.vector.quantize_mx(
+                out=e2_codes[:, g, cols].bitcast(FP8X4),
+                scales=e2_scales[:, g, cols],
+                in_=e2_grouped[:, g, cols, :].rearrange("p h j -> p (h j)"),
+            )
+
+        def scaled_sims(g):
+            cols = slice(g * BANK, (g + 1) * BANK)
+            nc.vector.tensor_tensor(out=x[:, cols], in0=dots[g][:], in1=scale[:, cols], op=ALU.mult)
+            nc.vector.tensor_reduce(out=part_max[:, g : g + 1], in_=x[:, cols], axis=ROW, op=ALU.max)
+
+        turn_features("q", q_rows[:])
+        copy_out(nc.vector.tensor_copy, "q", q_grouped[:])
+        nc.scalar.activation(
+            out=squares[:, CHUNKS, :], in_=q_rows[:], func=ACT.Square, accum_out=q_sq[:]
+        )
+        nc.gpsimd.tensor_tensor(out=q_norm[:], in0=q_sq[:], in1=half[:], op=ALU.pow)
+        nc.vector.quantize_mx(
+            out=q_codes[:].rearrange("p s r -> p (s r)").bitcast(FP8X4),
+            scales=q_scales[:].rearrange("p s r -> p (s r)"),
+            in_=q_grouped[:],
+        )
+        for c in range(VECTOR_COPIES):
+            turn_features(c, chunk_rows(c))
+            copy_out(nc.vector.tensor_copy, c, et_grouped[:, c, :])
+        spread = turn_ps.tile([P, P], F32, tag="turned")
+        nc.tensor.matmul(
+            out=spread[:], lhsT=q_norm[:, 0:1].to_broadcast([P, P]), rhs=ident[:], start=True, stop=True
+        )
+        for c in range(VECTOR_COPIES):
+            quantise_chunk(c)
+        nc.vector.tensor_scalar(
+            out=q_norm_cols[:], in0=spread[:], scalar1=1.0 / beta, scalar2=None, op0=ALU.mult
+        )
+
+        denominators(0)
+        for c in range(CHUNKS):
+            if VECTOR_COPIES <= c + 2 < CHUNKS:
+                turn_features(c + 2, chunk_rows(c + 2))
+            if c + 1 < CHUNKS:
+                denominators(c + 1)
+            if c >= VECTOR_COPIES:
+                copy_out(nc.scalar.copy, c, et_grouped[:, c, :])
+            if c >= PACK:
+                regroup(nc.scalar.copy, 1, c - PACK)
+            nc.vector.reciprocal(out=scale[:, c * P : (c + 1) * P], in_=den_bank(c))
+            if c >= VECTOR_COPIES:
+                quantise_chunk(c)
+            if c < PACK:
+                regroup(nc.vector.tensor_copy, 0, c)
+            if c == PACK:
                 scaled_sims(0)
-            if c % 2 == 0:
-                regroup(c // 4, (c // 2) % 2)
-            else:
-                quantise_words(c // 4, (c // 2) % 2)
-        invert(CHUNKS - 1)
         scaled_sims(1)
 
-        warm_exp = keep.tile([P, 1], F32)
-        nc.scalar.activation(
-            out=warm_exp[:], in_=e_norm[:, CHUNKS - 1 : CHUNKS], func=ACT.Exp, scale=0.0
-        )
-
         neg_max = keep.tile([P, 1], F32)
-        nc.vector.tensor_reduce(
-            out=neg_max[:], in_=part_max[:], axis=mybir.AxisListType.X, op=ALU.max, negate=True
-        )
+        nc.vector.tensor_reduce(out=neg_max[:], in_=part_max[:], axis=ROW, op=ALU.max, negate=True)
         prob = keep.tile([P, VOCAB], F32)
         part_sum = keep.tile([P, V_PASSES], F32)
         p_grouped = keep.tile([P, V_PASSES, QUERIES, PACK], BF16, align_bytes=64)
@@ -201,17 +206,21 @@ def tile_frozenhopfield_pa_s_kernel(tc, q, word_embs, beta, out):
                 out=prob[:, cols], in_=x[:, cols], func=ACT.Exp, bias=neg_max[:, 0:1], scale=1.0,
                 accum_out=part_sum[:, g : g + 1],
             )
+        quantise_words(0, 0)
+        quantise_words(0, 1)
+        quantise_words(1, 0)
+        p_turned = []
         for g in range(V_PASSES):
-            p_turned = turn_ps.tile([P, PACK, QUERIES], F32, tag="turned")
+            bank = turn_ps.tile([P, PACK, QUERIES], F32, tag="turned", name="p_turned%d" % g)
             for j in range(PACK):
                 first = (g * PACK + j) * P
-                nc.tensor.transpose(p_turned[:, j, :], prob[:, first : first + P], ident[:])
-            if g == 0:
-                nc.vector.tensor_copy(
-                    out=p_grouped[:, g, :, :], in_=p_turned[:].rearrange("p j b -> p b j")
-                )
-            else:
-                nc.scalar.copy(out=p_grouped[:, g, :, :], in_=p_turned[:].rearrange("p j b -> p b j"))
+                nc.tensor.transpose(bank[:, j, :], prob[:, first : first + P], ident[:])
+            p_turned.append(bank)
+        nc.vector.tensor_copy(
+            out=p_grouped[:, 0, :, :], in_=p_turned[0][:].rearrange("p j b -> p b j")
+        )
+        nc.scalar.copy(out=p_grouped[:, 1, :, :], in_=p_turned[1][:].rearrange("p j b -> p b j"))
+        quantise_words(1, 1)
         for g in range(V_PASSES):
             nc.vector.quantize_mx(
                 out=p_codes[:, g, :].bitcast(FP8X4),
@@ -219,18 +228,17 @@ def tile_frozenhopfield_pa_s_kernel(tc, q, word_embs, beta, out):
                 in_=p_grouped[:, g, :, :].rearrange("p b j -> p (b j)"),
             )
         row_sum = keep.tile([P, 1], F32)
-        nc.vector.tensor_reduce(
-            out=row_sum[:], in_=part_sum[:], axis=mybir.AxisListType.X, op=ALU.add
-        )
+        nc.vector.tensor_reduce(out=row_sum[:], in_=part_sum[:], axis=ROW, op=ALU.add)
         inv_sum = keep.tile([P, 1], F32)
         nc.vector.reciprocal(out=inv_sum[:], in_=row_sum[:])
 
-        for n in range(HID // BANK):
-            cols = slice(n * BANK, (n + 1) * BANK)
-            acc = hold_ps.tile([P, BANK], F32, name="acc%d" % n, tag="dots%d" % n)
-            for g in range(V_PASSES):
+        halves = range(HID // BANK)
+        acc = [hold_ps.tile([P, BANK], F32, name="acc%d" % n, tag="dots%d" % n) for n in halves]
+        for g in range(V_PASSES):
+            for n in halves:
+                cols = slice(n * BANK, (n + 1) * BANK)
                 nc.tensor.matmul_mx(
-                    out=acc[:],
+                    out=acc[n][:],
                     lhsT=p_codes[:, g, :].bitcast(FP8X4),
                     lhsT_scale=p_scales[:, g, :],
                     rhs=e2_codes[:, g, cols].bitcast(FP8X4),
@@ -238,12 +246,10 @@ def tile_frozenhopfield_pa_s_kernel(tc, q, word_embs, beta, out):
                     start=(g == 0),
                     stop=(g == V_PASSES - 1),
                 )
-            result = keep.tile([P, BANK], F32, name="result%d" % n)
-            if n == 0:
-                nc.vector.tensor_scalar(
-                    out=result[:], in0=acc[:], scalar1=inv_sum[:, 0:1], scalar2=None, op0=ALU.mult
-                )
-                nc.sync.dma_start(out=out[:, cols], in_=result[:])
-            else:
-                nc.scalar.activation(out=result[:], in_=acc[:], func=ACT.Copy, scale=inv_sum[:, 0:1])
-                nc.scalar.dma_start(out=out[:, cols], in_=result[:])
+        result = [keep.tile([P, BANK], F32, name="result%d" % n) for n in halves]
+        nc.vector.tensor_scalar(
+            out=result[0][:], in0=acc[0][:], scalar1=inv_sum[:, 0:1], scalar2=None, op0=ALU.mult
+        )
+        nc.sync.dma_start(out=out[:, 0:BANK], in_=result[0][:])
+        nc.scalar.activation(out=result[1][:], in_=acc[1][:], func=ACT.Copy, scale=inv_sum[:, 0:1])
+        nc.scalar.dma_start(out=out[:, BANK : 2 * BANK], in_=result[1][:])

from contextlib import ExitStack

import concourse.mybir as mybir
from concourse.masks import make_identity

F32 = mybir.dt.float32
BF16 = mybir.dt.bfloat16
U32 = mybir.dt.uint32
U8 = mybir.dt.uint8
FP8X4 = mybir.dt.float8_e4m3fn_x4
ALU = mybir.AluOpType
ACT = mybir.ActivationFunctionType
ROW = mybir.AxisListType.X

P = 128
PACK = 4
K_PASS = P * PACK
QUERIES = 128
HID = 1024
VOCAB = 1024
H_PASSES = HID // K_PASS
V_PASSES = VOCAB // K_PASS
CHUNKS = VOCAB // P
BANK = 512
QUARTER = HID // PACK
EPS = 1e-8
VECTOR_COPIES = 2

FLOPS = 2 * 2 * QUERIES * VOCAB * HID


def tile_frozenhopfield_pa_s_kernel(tc, q, word_embs, beta, out):
    nc = tc.nc
    with ExitStack() as pools:
        keep = pools.enter_context(tc.tile_pool(name="keep", bufs=1))
        turn_ps = pools.enter_context(tc.psum_pool(name="turn_ps", bufs=4))
        hold_ps = pools.enter_context(tc.psum_pool(name="hold_ps", bufs=1))
        pools.enter_context(tc.manual_schedule())

        q_rows = keep.tile([P, HID], BF16, align_bytes=64)
        nc.sync.dma_start(out=q_rows[:], in_=q[:, :])
        e_rows = keep.tile([P, V_PASSES, PACK, HID], BF16, align_bytes=64)
        e_dram = word_embs.rearrange("(g p j) h -> p g j h", g=V_PASSES, p=P, j=PACK)
        for g in range(V_PASSES):
            for j in range(PACK):
                nc.sync.dma_start(out=e_rows[:, g, j, :], in_=e_dram[:, g, j, :])

        ident = keep.tile([P, P], F32)
        make_identity(nc, ident[:])
        half = keep.tile([P, 1], F32)
        nc.gpsimd.memset(half[:], 0.5)

        warm = keep.tile([P, 1], F32)
        nc.vector.memset(warm[:], 0.0)
        nc.scalar.activation(out=warm[:], in_=warm[:], func=ACT.Exp)

        squares = keep.tile([P, CHUNKS + 1, HID], BF16)
        q_sq = keep.tile([P, 1], F32)
        q_norm = keep.tile([P, 1], F32)
        e_sq = keep.tile([P, CHUNKS], F32)
        e_norm = keep.tile([P, CHUNKS], F32)

        q_grouped = keep.tile([P, HID], BF16, align_bytes=64)
        q_codes = keep.tile([P, H_PASSES, P], U32, align_bytes=64)
        q_scales = keep.tile([P, H_PASSES, P], U8, align_bytes=64)
        et_grouped = keep.tile([P, CHUNKS, HID], BF16, align_bytes=64)
        et_codes = keep.tile([P, CHUNKS, H_PASSES, P], U32, align_bytes=64)
        et_scales = keep.tile([P, CHUNKS, H_PASSES, P], U8, align_bytes=64)
        e2_grouped = keep.tile([P, V_PASSES, HID, PACK], BF16, align_bytes=64)
        e2_codes = keep.tile([P, V_PASSES, HID], U32, align_bytes=64)
        e2_scales = keep.tile([P, V_PASSES, HID], U8, align_bytes=64)

        q_norm_cols = keep.tile([P, QUERIES], F32)
        dots = [hold_ps.tile([P, BANK], F32, name="dots%d" % g) for g in range(V_PASSES)]
        dens = [hold_ps.tile([P, BANK], F32, name="dens%d" % i) for i in range(2)]
        den_t = keep.tile([P, CHUNKS, QUERIES], F32)
        scale = keep.tile([P, VOCAB], F32)
        x = keep.tile([P, VOCAB], F32)
        part_max = keep.tile([P, V_PASSES], F32)
        turned = {}

        def chunk_rows(c):
            return e_rows[:, c // PACK, c % PACK, :]

        def turn_features(name, rows):
            words = rows.bitcast(F32)
            bank = turn_ps.tile([P, H_PASSES, 2, P], F32, tag="turned", name="turned_%s" % name)
            for s in range(H_PASSES):
                for u in range(2):
                    first = (2 * s + u) * P
                    nc.tensor.transpose(bank[:, s, u, :], words[:, first : first + P], ident[:])
            turned[name] = bank

        def copy_out(copy, name, grouped):
            copy(
                out=grouped.bitcast(F32).rearrange("p (s r u) -> p s r u", s=H_PASSES, u=2),
                in_=turned[name][:].rearrange("p s u r -> p s r u"),
            )

        def quantise_chunk(c):
            nc.vector.quantize_mx(
                out=et_codes[:, c, :, :].rearrange("p s r -> p (s r)").bitcast(FP8X4),
                scales=et_scales[:, c, :, :].rearrange("p s r -> p (s r)"),
                in_=et_grouped[:, c, :],
            )
            for s in range(H_PASSES):
                nc.tensor.matmul_mx(
                    out=dots[c // PACK][:, (c % PACK) * P : (c % PACK + 1) * P],
                    lhsT=q_codes[:, s, :].bitcast(FP8X4),
                    lhsT_scale=q_scales[:, s, :],
                    rhs=et_codes[:, c, s, :].bitcast(FP8X4),
                    rhs_scale=et_scales[:, c, s, :],
                    start=(s == 0),
                    stop=(s == H_PASSES - 1),
                )

        def den_bank(c):
            return dens[c % 2][:, (c // 2) * P : (c // 2 + 1) * P]

        def denominators(c):
            nc.scalar.activation(
                out=squares[:, c, :], in_=chunk_rows(c), func=ACT.Square, accum_out=e_sq[:, c : c + 1]
            )
            nc.gpsimd.tensor_tensor(
                out=e_norm[:, c : c + 1], in0=e_sq[:, c : c + 1], in1=half[:], op=ALU.pow
            )
            nc.gpsimd.tensor_scalar(
                out=den_t[:, c, :], in0=q_norm_cols[:], scalar1=e_norm[:, c : c + 1],
                scalar2=EPS / beta, op0=ALU.mult, op1=ALU.add,
            )
            nc.tensor.transpose(den_bank(c), den_t[:, c, :], ident[:])

        def regroup(copy, g, part):
            cols = slice(part * QUARTER, (part + 1) * QUARTER)
            copy(
                out=e2_grouped[:, g, cols, :].rearrange("p (c i) j -> p c j i", i=4),
                in_=e_rows[:, g, :, cols].rearrange("p j (c i) -> p c j i", i=4),
            )

        def quantise_words(g, n):
            cols = slice(n * BANK, (n + 1) * BANK)
            nc.vector.quantize_mx(
                out=e2_codes[:, g, cols].bitcast(FP8X4),
                scales=e2_scales[:, g, cols],
                in_=e2_grouped[:, g, cols, :].rearrange("p h j -> p (h j)"),
            )

        def scaled_sims(g):
            cols = slice(g * BANK, (g + 1) * BANK)
            nc.vector.tensor_tensor(out=x[:, cols], in0=dots[g][:], in1=scale[:, cols], op=ALU.mult)
            nc.vector.tensor_reduce(out=part_max[:, g : g + 1], in_=x[:, cols], axis=ROW, op=ALU.max)

        turn_features("q", q_rows[:])
        copy_out(nc.vector.tensor_copy, "q", q_grouped[:])
        nc.scalar.activation(
            out=squares[:, CHUNKS, :], in_=q_rows[:], func=ACT.Square, accum_out=q_sq[:]
        )
        nc.gpsimd.tensor_tensor(out=q_norm[:], in0=q_sq[:], in1=half[:], op=ALU.pow)
        nc.vector.quantize_mx(
            out=q_codes[:].rearrange("p s r -> p (s r)").bitcast(FP8X4),
            scales=q_scales[:].rearrange("p s r -> p (s r)"),
            in_=q_grouped[:],
        )
        for c in range(VECTOR_COPIES):
            turn_features(c, chunk_rows(c))
            copy_out(nc.vector.tensor_copy, c, et_grouped[:, c, :])
        spread = turn_ps.tile([P, P], F32, tag="turned")
        nc.tensor.matmul(
            out=spread[:], lhsT=q_norm[:, 0:1].to_broadcast([P, P]), rhs=ident[:], start=True, stop=True
        )
        for c in range(VECTOR_COPIES):
            quantise_chunk(c)
        nc.vector.tensor_scalar(
            out=q_norm_cols[:], in0=spread[:], scalar1=1.0 / beta, scalar2=None, op0=ALU.mult
        )

        denominators(0)
        for c in range(CHUNKS):
            if VECTOR_COPIES <= c + 2 < CHUNKS:
                turn_features(c + 2, chunk_rows(c + 2))
            if c + 1 < CHUNKS:
                denominators(c + 1)
            if c >= VECTOR_COPIES:
                copy_out(nc.scalar.copy, c, et_grouped[:, c, :])
            if c >= PACK:
                regroup(nc.scalar.copy, 1, c - PACK)
            nc.vector.reciprocal(out=scale[:, c * P : (c + 1) * P], in_=den_bank(c))
            if c >= VECTOR_COPIES:
                quantise_chunk(c)
            if c < PACK:
                regroup(nc.vector.tensor_copy, 0, c)
            if c == PACK:
                scaled_sims(0)
        scaled_sims(1)

        neg_max = keep.tile([P, 1], F32)
        nc.vector.tensor_reduce(out=neg_max[:], in_=part_max[:], axis=ROW, op=ALU.max, negate=True)
        prob = keep.tile([P, VOCAB], F32)
        part_sum = keep.tile([P, V_PASSES], F32)
        p_grouped = keep.tile([P, V_PASSES, QUERIES, PACK], BF16, align_bytes=64)
        p_codes = keep.tile([P, V_PASSES, QUERIES], U32, align_bytes=64)
        p_scales = keep.tile([P, V_PASSES, QUERIES], U8, align_bytes=64)
        for g in range(V_PASSES):
            cols = slice(g * BANK, (g + 1) * BANK)
            nc.scalar.activation(
                out=prob[:, cols], in_=x[:, cols], func=ACT.Exp, bias=neg_max[:, 0:1], scale=1.0,
                accum_out=part_sum[:, g : g + 1],
            )
        quantise_words(0, 0)
        quantise_words(0, 1)
        quantise_words(1, 0)
        p_turned = []
        for g in range(V_PASSES):
            bank = turn_ps.tile([P, PACK, QUERIES], F32, tag="turned", name="p_turned%d" % g)
            for j in range(PACK):
                first = (g * PACK + j) * P
                nc.tensor.transpose(bank[:, j, :], prob[:, first : first + P], ident[:])
            p_turned.append(bank)
        nc.vector.tensor_copy(
            out=p_grouped[:, 0, :, :], in_=p_turned[0][:].rearrange("p j b -> p b j")
        )
        nc.scalar.copy(out=p_grouped[:, 1, :, :], in_=p_turned[1][:].rearrange("p j b -> p b j"))
        quantise_words(1, 1)
        for g in range(V_PASSES):
            nc.vector.quantize_mx(
                out=p_codes[:, g, :].bitcast(FP8X4),
                scales=p_scales[:, g, :],
                in_=p_grouped[:, g, :, :].rearrange("p b j -> p (b j)"),
            )
        row_sum = keep.tile([P, 1], F32)
        nc.vector.tensor_reduce(out=row_sum[:], in_=part_sum[:], axis=ROW, op=ALU.add)
        inv_sum = keep.tile([P, 1], F32)
        nc.vector.reciprocal(out=inv_sum[:], in_=row_sum[:])

        halves = range(HID // BANK)
        acc = [hold_ps.tile([P, BANK], F32, name="acc%d" % n, tag="dots%d" % n) for n in halves]
        for g in range(V_PASSES):
            for n in halves:
                cols = slice(n * BANK, (n + 1) * BANK)
                nc.tensor.matmul_mx(
                    out=acc[n][:],
                    lhsT=p_codes[:, g, :].bitcast(FP8X4),
                    lhsT_scale=p_scales[:, g, :],
                    rhs=e2_codes[:, g, cols].bitcast(FP8X4),
                    rhs_scale=e2_scales[:, g, cols],
                    start=(g == 0),
                    stop=(g == V_PASSES - 1),
                )
        result = [keep.tile([P, BANK], F32, name="result%d" % n) for n in halves]
        nc.vector.tensor_scalar(
            out=result[0][:], in0=acc[0][:], scalar1=inv_sum[:, 0:1], scalar2=None, op0=ALU.mult
        )
        nc.sync.dma_start(out=out[:, 0:BANK], in_=result[0][:])
        nc.scalar.activation(out=result[1][:], in_=acc[1][:], func=ACT.Copy, scale=inv_sum[:, 0:1])
        nc.scalar.dma_start(out=out[:, BANK : 2 * BANK], in_=result[1][:])
